import numpy as np
import ml_dtypes


def mxq(x, axis, fmt="e4m3"):
    dtype, down = {"e4m3": (ml_dtypes.float8_e4m3fn, 7), "e5m2": (ml_dtypes.float8_e5m2, 14)}[fmt]
    v = np.moveaxis(np.asarray(x, np.float32).astype(ml_dtypes.bfloat16).astype(np.float64), axis, -1)
    blocks = v.reshape(v.shape[:-1] + (-1, 32))
    amax = np.abs(blocks).max(-1, keepdims=True)
    byte = np.maximum(np.where(amax > 0, np.frexp(amax)[1] - 1 + 127, 0) - down, 1)
    scale = np.exp2(byte - 127.0)
    codes = (blocks / scale).astype(np.float32).astype(dtype).astype(np.float64)
    return np.moveaxis((codes * scale).reshape(v.shape), -1, axis)


WIDE = False


def mx_kscale(k):
    if not WIDE:
        return np.ones(k)
    levels = np.array([10, -10, 5, -5, 0])
    if k % 512:
        return np.exp2(np.random.permutation(np.resize(levels, k // 32))).repeat(32)
    a = np.empty((k // 512, 16))
    for p in range(k // 512):
        a[p, :8] = np.random.permutation(np.resize(levels, 8))
        for g in range(8):
            far = levels[np.abs(levels - a[p, g]) >= 10]
            a[p, g + 8] = far[np.random.randint(len(far))]
    return np.exp2(a.ravel()).repeat(32)


BF16 = ml_dtypes.bfloat16


def bf(x):
    return np.asarray(x, np.float32).astype(BF16)


def f64(x):
    return np.asarray(x).astype(np.float64)


B, K, N = 2048, 512, 1024
NACT = 4


def setup_inputs():
    s = mx_kscale(K)
    g = np.tile(np.array([1.0, 1.0, 1.0, 0.5]), N // NACT)
    x = np.random.standard_normal((B, K)) * s
    weight = np.random.uniform(-1.0, 1.0, (N, K)) / np.sqrt(K) * g[:, None] / s[None, :]
    return {"x": bf(x), "weight": bf(weight)}


def reference(x, weight):
    y = mxq(f64(x), 1, "e4m3") @ mxq(f64(weight), 1, "e4m3").T
    rows, cols = y.shape
    y3 = y.reshape(rows, cols // NACT, NACT)
    out = np.stack(
        [y3[..., 0],
         np.cos(y3[..., 1]),
         np.sin(y3[..., 2]),
         np.tan(y3[..., 3])],
        axis=-1,
    )
    return out.reshape(rows, cols)

@@ -1,0 +1,282 @@
+import math
+from contextlib import ExitStack
+
+import concourse.mybir as mybir
+from concourse.masks import make_identity
+
+FLOPS = 2 * 2048 * 512 * 1024
+
+F32 = mybir.dt.float32
+BF16 = mybir.dt.bfloat16
+U32 = mybir.dt.uint32
+U8 = mybir.dt.uint8
+FP8X4 = mybir.dt.float8_e4m3fn_x4
+ACT = mybir.ActivationFunctionType
+MULT = mybir.AluOpType.mult
+
+P = 128
+K = 512
+ROW_WORDS = K // 2
+PACK = 4
+ROW_TILES = 16
+BATCHES = 4
+LINEAR = 0
+COS = 1
+SIN = 2
+TAN = 3
+CLASSES = 4
+CLASS_COLS = 256
+OUT_COLS = CLASSES * CLASS_COLS
+PLANE = 2 * CLASS_COLS
+BANK = 512
+assert PLANE == BANK
+
+
+def tile_mylayerfunc_kernel(tc, x, weight, out):
+    nc = tc.nc
+    with ExitStack() as ctx:
+        keep = ctx.enter_context(tc.tile_pool(name="keep", bufs=1))
+        work = ctx.enter_context(tc.tile_pool(name="work", bufs=2))
+        psum = ctx.enter_context(tc.psum_pool(name="psum", bufs=8))
+
+        zero = keep.tile([P, 1], F32, name="zero")
+        half_pi = keep.tile([P, 1], F32, name="half_pi")
+        warm = keep.tile([P, 1], F32, name="warm")
+        ident = keep.tile([P, P], F32, name="ident")
+        nc.vector.memset(zero[:], 0.0)
+        nc.vector.tensor_scalar_add(out=half_pi[:], in0=zero[:], scalar1=math.pi / 2)
+        nc.scalar.activation(out=warm[:], in_=half_pi[:], func=ACT.Sin)
+        make_identity(nc, ident[:])
+
+        w_raw = keep.tile([P, CLASSES * 2 * K], BF16, name="w_raw")
+        x_raw = keep.tile([P, ROW_TILES * K], BF16, name="x_raw")
+        w_view = weight.rearrange("(h p c) k -> c p h k", h=2, p=P, c=CLASSES)
+        x_view = x.rearrange("(p r) k -> p (r k)", r=ROW_TILES)
+
+        def load_weight(c):
+            nc.sync.dma_start(
+                out=w_raw[:, c * 2 * K:(c + 1) * 2 * K].rearrange("p (h k) -> p h k", h=2), in_=w_view[c]
+            )
+
+        def load_x(first_tile, end_tile):
+            nc.sync.dma_start(
+                out=x_raw[:, first_tile * K:end_tile * K], in_=x_view[:, first_tile * K:end_tile * K]
+            )
+
+        load_weight(TAN)
+        load_x(0, 2)
+        load_x(2, 4)
+        load_x(4, 8)
+        load_weight(COS)
+        load_weight(SIN)
+        load_weight(LINEAR)
+        load_x(8, 12)
+        load_x(12, 16)
+        w_words = w_raw[:].bitcast(F32)
+        x_words = x_raw[:].bitcast(F32)
+
+        w_grp = keep.tile([P, OUT_COLS * PACK], BF16, name="w_grp", align_bytes=64)
+        x_grp = keep.tile([P, ROW_TILES * P * PACK], BF16, name="x_grp", align_bytes=64)
+        w_grp_words = w_grp[:].bitcast(F32)
+        x_grp_words = x_grp[:].bitcast(F32)
+        w_codes = keep.tile([P, OUT_COLS], U32, name="w_codes", align_bytes=64)
+        w_scales = keep.tile([P, OUT_COLS], U8, name="w_scales", align_bytes=64)
+        x_codes = keep.tile([P, ROW_TILES * P], U32, name="x_codes", align_bytes=64)
+        x_scales = keep.tile([P, ROW_TILES * P], U8, name="x_scales", align_bytes=64)
+
+        def transpose_to_bank(words, first_word, label):
+            bank = psum.tile([P, BANK], F32, name=label, tag="bank")
+            halves = bank[:].rearrange("p (u n) -> p u n", u=2)
+            for blk in range(2):
+                for u in range(2):
+                    lo = first_word + blk * ROW_WORDS
+                    nc.tensor.transpose(
+                        halves[:, u, blk * P:(blk + 1) * P], words[:, lo + u:lo + ROW_WORDS:2], ident[:]
+                    )
+            return bank
+
+        def regroup(on_vector, bank, dst_words):
+            dst = dst_words.rearrange("p (n u) -> p n u", u=2)
+            src = bank[:].rearrange("p (u n) -> p n u", u=2)
+            if on_vector:
+                nc.vector.tensor_copy(out=dst, in_=src)
+            else:
+                nc.scalar.copy(out=dst, in_=src)
+
+        w_banks = {}
+        x_banks = {}
+
+        def transpose_weight(c):
+            w_banks[c] = transpose_to_bank(w_words, c * 2 * ROW_WORDS, "wt%d" % c)
+
+        def transpose_x(q):
+            x_banks[q] = transpose_to_bank(x_words, q * 2 * ROW_WORDS, "xt%d" % q)
+
+        def regroup_weight(c, on_vector):
+            regroup(on_vector, w_banks[c], w_grp_words[:, c * BANK:(c + 1) * BANK])
+
+        def regroup_x(q, on_vector):
+            regroup(on_vector, x_banks[q], x_grp_words[:, q * BANK:(q + 1) * BANK])
+
+        def quantise_weight(c):
+            nc.vector.quantize_mx(
+                out=w_codes[:, c * CLASS_COLS:(c + 1) * CLASS_COLS].bitcast(FP8X4),
+                scales=w_scales[:, c * CLASS_COLS:(c + 1) * CLASS_COLS],
+                in_=w_grp[:, c * CLASS_COLS * PACK:(c + 1) * CLASS_COLS * PACK],
+            )
+
+        def quantise_x(first_pair, pairs):
+            lo = first_pair * 2 * P
+            hi = (first_pair + pairs) * 2 * P
+            nc.vector.quantize_mx(
+                out=x_codes[:, lo:hi].bitcast(FP8X4),
+                scales=x_scales[:, lo:hi],
+                in_=x_grp[:, PACK * lo:PACK * hi],
+            )
+
+        def multiply(q, c):
+            bank = psum.tile([P, BANK], F32, name="y%d_%d" % (c, q), tag="bank")
+            for t in range(2):
+                r = 2 * q + t
+                nc.tensor.matmul_mx(
+                    out=bank[:, t * CLASS_COLS:(t + 1) * CLASS_COLS],
+                    lhsT=x_codes[:, r * P:(r + 1) * P].bitcast(FP8X4),
+                    lhsT_scale=x_scales[:, r * P:(r + 1) * P],
+                    rhs=w_codes[:, c * CLASS_COLS:(c + 1) * CLASS_COLS].bitcast(FP8X4),
+                    rhs_scale=w_scales[:, c * CLASS_COLS:(c + 1) * CLASS_COLS],
+                    start=True,
+                    stop=True,
+                )
+            return bank
+
+        out_view = out.rearrange("(p r) j -> p (r j)", r=ROW_TILES)
+        y_tan = {}
+        y_rest = {}
+        cosines = {}
+        sines = {}
+        planes = {}
+        woven = {}
+
+        def multiply_tan(q):
+            y_tan[q] = multiply(q, TAN)
+
+        def multiply_rest(q):
+            y_rest[q] = [multiply(q, COS), multiply(q, SIN), multiply(q, LINEAR)]
+
+        def tan_inputs(b):
+            cosines[b] = work.tile([P, 2, PLANE], F32, name="cos3_%d" % b, tag="cos3")
+            sines[b] = work.tile([P, 2, PLANE], F32, name="sin3_%d" % b, tag="sin3")
+            planes[b] = work.tile([P, 2, CLASSES, PLANE], F32, name="res_%d" % b, tag="res", bufs=3)
+            magnitudes = work.tile([P, 2, PLANE], F32, name="abs3_%d" % b, tag="abs3")
+            y_first = y_tan[2 * b]
+            y_second = y_tan[2 * b + 1]
+            nc.scalar.activation(out=magnitudes[:, 0, :], in_=y_first[:], func=ACT.Abs)
+            nc.scalar.activation(out=sines[b][:, 1, :], in_=y_first[:], func=ACT.Sin)
+            nc.scalar.activation(out=magnitudes[:, 1, :], in_=y_second[:], func=ACT.Abs)
+            nc.scalar.activation(out=sines[b][:, 0, :], in_=y_second[:], func=ACT.Sin)
+            nc.scalar.activation(out=cosines[b][:], in_=magnitudes[:], func=ACT.Sin, scale=-1.0, bias=half_pi[:])
+
+        def other_classes(q):
+            b = q // 2
+            slot = 1 - q % 2
+            y_cos, y_sin, y_linear = y_rest[q]
+            magnitude = work.tile([P, PLANE], F32, name="abs1_%d" % q, tag="abs1")
+            nc.scalar.activation(out=magnitude[:], in_=y_cos[:], func=ACT.Abs)
+            nc.scalar.activation(out=planes[b][:, slot, SIN, :], in_=y_sin[:], func=ACT.Sin)
+            nc.scalar.activation(
+                out=planes[b][:, slot, COS, :], in_=magnitude[:], func=ACT.Sin, scale=-1.0, bias=half_pi[:]
+            )
+            nc.scalar.copy(out=planes[b][:, slot, LINEAR, :], in_=y_linear[:])
+
+        def weave_and_store(b, step):
+            q = 2 * b + step // 2
+            t = step % 2
+            slot = 1 - step // 2
+            if t == 0:
+                woven[q] = work.tile([P, 2 * OUT_COLS], F32, name="o_%d" % q, tag="o", bufs=4)
+            rows = woven[q][:, t * OUT_COLS:(t + 1) * OUT_COLS]
+            nc.vector.tensor_copy(
+                out=rows.rearrange("p (g e c) -> p g c e", e=4, c=CLASSES),
+                in_=planes[b][:, slot, :, t * CLASS_COLS:(t + 1) * CLASS_COLS].rearrange("p c (g e) -> p g c e", e=4),
+            )
+            r = 2 * q + t
+            nc.sync.dma_start(out=out_view[:, r * OUT_COLS:(r + 1) * OUT_COLS], in_=rows)
+
+        def mul(dst, left, right):
+            nc.vector.tensor_tensor(out=dst, in0=left, in1=right, op=MULT)
+
+        def divide(b):
+            cs = cosines[b]
+            sn = sines[b]
+            half = PLANE // 2
+            quarter = PLANE // 4
+            p1 = work.tile([P, PLANE], F32, name="p1_%d" % b, tag="p1")
+            p2 = work.tile([P, half], F32, name="p2_%d" % b, tag="p2")
+            p3 = work.tile([P, quarter], F32, name="p3_%d" % b, tag="p3")
+            r3 = work.tile([P, quarter], F32, name="r3_%d" % b, tag="r3")
+            r2 = work.tile([P, half], F32, name="r2_%d" % b, tag="r2")
+            r1 = work.tile([P, PLANE], F32, name="r1_%d" % b, tag="r1")
+            num = work.tile([P, 2, PLANE], F32, name="num_%d" % b, tag="num")
+            mul(p1[:], cs[:, 0, :], cs[:, 1, :])
+            mul(num[:, 0, :], sn[:, 0, :], cs[:, 0, :])
+            mul(p2[:], p1[:, 0:half], p1[:, half:PLANE])
+            mul(num[:, 1, :], sn[:, 1, :], cs[:, 1, :])
+            mul(p3[:], p2[:, 0:quarter], p2[:, quarter:half])
+            nc.vector.reciprocal(out=r3[:], in_=p3[:])
+            mul(r2[:, 0:quarter], r3[:], p2[:, quarter:half])
+            mul(r2[:, quarter:half], r3[:], p2[:, 0:quarter])
+            mul(r1[:, 0:half], r2[:], p1[:, half:PLANE])
+            mul(r1[:, half:PLANE], r2[:], p1[:, 0:half])
+            mul(planes[b][:, :, TAN, :], num[:], r1[:].unsqueeze(1).to_broadcast([P, 2, PLANE]))
+
+        transpose_weight(TAN)
+        transpose_x(0)
+        transpose_x(1)
+        regroup_weight(TAN, True)
+        regroup_x(0, False)
+        quantise_weight(TAN)
+        quantise_x(0, 1)
+        multiply_tan(0)
+        transpose_x(2)
+        transpose_x(3)
+        regroup_x(1, True)
+        regroup_x(2, True)
+        quantise_x(1, 1)
+        multiply_tan(1)
+        transpose_weight(COS)
+        transpose_weight(SIN)
+        transpose_weight(LINEAR)
+        tan_inputs(0)
+        regroup_x(3, True)
+        regroup_weight(COS, True)
+        quantise_x(2, 2)
+        multiply_tan(2)
+        multiply_tan(3)
+        regroup_weight(SIN, False)
+        regroup_weight(LINEAR, False)
+        quantise_weight(COS)
+        quantise_weight(SIN)
+        quantise_weight(LINEAR)
+        divide(0)
+
+        for b in range(BATCHES):
+            ahead = b + 1
+            if ahead < BATCHES:
+                tan_inputs(ahead)
+            if ahead + 1 < BATCHES:
+                transpose_x(2 * ahead + 2)
+                transpose_x(2 * ahead + 3)
+                regroup_x(2 * ahead + 2, False)
+                regroup_x(2 * ahead + 3, False)
+            multiply_rest(2 * b)
+            multiply_rest(2 * b + 1)
+            other_classes(2 * b)
+            other_classes(2 * b + 1)
+            if ahead + 1 < BATCHES:
+                quantise_x(2 * ahead + 2, 2)
+                multiply_tan(2 * ahead + 2)
+                multiply_tan(2 * ahead + 3)
+            if ahead < BATCHES:
+                divide(ahead)
+            for step in range(4):
+                weave_and_store(b, step)

@@ -19,7 +19,7 @@ K = 512
 ROW_WORDS = K // 2
 PACK = 4
 ROW_TILES = 16
-BATCHES = 4
+BATCH_PAIRS = ((0,), (1, 2), (3, 4), (5, 6), (7,))
 LINEAR = 0
 COS = 1
 SIN = 2
@@ -38,6 +38,7 @@ def tile_mylayerfunc_kernel(tc, x, weight, out):
         keep = ctx.enter_context(tc.tile_pool(name="keep", bufs=1))
         work = ctx.enter_context(tc.tile_pool(name="work", bufs=2))
         psum = ctx.enter_context(tc.psum_pool(name="psum", bufs=8))
+        ctx.enter_context(tc.manual_schedule())
 
         zero = keep.tile([P, 1], F32, name="zero")
         half_pi = keep.tile([P, 1], F32, name="half_pi")
@@ -64,14 +65,13 @@ def tile_mylayerfunc_kernel(tc, x, weight, out):
             )
 
         load_weight(TAN)
-        load_x(0, 2)
-        load_x(2, 4)
-        load_x(4, 8)
+        for q in range(3):
+            load_x(2 * q, 2 * q + 2)
         load_weight(COS)
         load_weight(SIN)
         load_weight(LINEAR)
-        load_x(8, 12)
-        load_x(12, 16)
+        load_x(6, 10)
+        load_x(10, 16)
         w_words = w_raw[:].bitcast(F32)
         x_words = x_raw[:].bitcast(F32)
 
@@ -155,128 +155,150 @@ def tile_mylayerfunc_kernel(tc, x, weight, out):
         cosines = {}
         sines = {}
         planes = {}
-        woven = {}
 
         def multiply_tan(q):
             y_tan[q] = multiply(q, TAN)
 
         def multiply_rest(q):
             y_rest[q] = [multiply(q, COS), multiply(q, SIN), multiply(q, LINEAR)]
+            planes[q] = work.tile([P, CLASSES, PLANE], F32, name="res_%d" % q, tag="res", bufs=6)
 
         def tan_inputs(b):
-            cosines[b] = work.tile([P, 2, PLANE], F32, name="cos3_%d" % b, tag="cos3")
-            sines[b] = work.tile([P, 2, PLANE], F32, name="sin3_%d" % b, tag="sin3")
-            planes[b] = work.tile([P, 2, CLASSES, PLANE], F32, name="res_%d" % b, tag="res", bufs=3)
-            magnitudes = work.tile([P, 2, PLANE], F32, name="abs3_%d" % b, tag="abs3")
-            y_first = y_tan[2 * b]
-            y_second = y_tan[2 * b + 1]
-            nc.scalar.activation(out=magnitudes[:, 0, :], in_=y_first[:], func=ACT.Abs)
-            nc.scalar.activation(out=sines[b][:, 1, :], in_=y_first[:], func=ACT.Sin)
-            nc.scalar.activation(out=magnitudes[:, 1, :], in_=y_second[:], func=ACT.Abs)
-            nc.scalar.activation(out=sines[b][:, 0, :], in_=y_second[:], func=ACT.Sin)
+            pairs = BATCH_PAIRS[b]
+            n = len(pairs) * PLANE
+            cosines[b] = work.tile([P, n], F32, name="cos3_%d" % b, tag="cos3")
+            sines[b] = work.tile([P, n], F32, name="sin3_%d" % b, tag="sin3")
+            magnitudes = work.tile([P, n], F32, name="abs3_%d" % b, tag="abs3")
+            for j, q in enumerate(pairs):
+                cols = slice(j * PLANE, (j + 1) * PLANE)
+                nc.scalar.activation(out=magnitudes[:, cols], in_=y_tan[q][:], func=ACT.Abs)
+                nc.scalar.activation(out=sines[b][:, cols], in_=y_tan[q][:], func=ACT.Sin)
             nc.scalar.activation(out=cosines[b][:], in_=magnitudes[:], func=ACT.Sin, scale=-1.0, bias=half_pi[:])
 
         def other_classes(q):
-            b = q // 2
-            slot = 1 - q % 2
             y_cos, y_sin, y_linear = y_rest[q]
             magnitude = work.tile([P, PLANE], F32, name="abs1_%d" % q, tag="abs1")
             nc.scalar.activation(out=magnitude[:], in_=y_cos[:], func=ACT.Abs)
-            nc.scalar.activation(out=planes[b][:, slot, SIN, :], in_=y_sin[:], func=ACT.Sin)
-            nc.scalar.activation(
-                out=planes[b][:, slot, COS, :], in_=magnitude[:], func=ACT.Sin, scale=-1.0, bias=half_pi[:]
-            )
-            nc.scalar.copy(out=planes[b][:, slot, LINEAR, :], in_=y_linear[:])
+            nc.scalar.activation(out=planes[q][:, SIN, :], in_=y_sin[:], func=ACT.Sin)
+            nc.scalar.activation(out=planes[q][:, COS, :], in_=magnitude[:], func=ACT.Sin, scale=-1.0, bias=half_pi[:])
+            nc.scalar.copy(out=planes[q][:, LINEAR, :], in_=y_linear[:])
 
-        def weave_and_store(b, step):
-            q = 2 * b + step // 2
-            t = step % 2
-            slot = 1 - step // 2
-            if t == 0:
-                woven[q] = work.tile([P, 2 * OUT_COLS], F32, name="o_%d" % q, tag="o", bufs=4)
-            rows = woven[q][:, t * OUT_COLS:(t + 1) * OUT_COLS]
+        def weave_and_store(q, t):
+            rows = work.tile([P, OUT_COLS], F32, name="o_%d_%d" % (q, t), tag="o", bufs=6)
             nc.vector.tensor_copy(
-                out=rows.rearrange("p (g e c) -> p g c e", e=4, c=CLASSES),
-                in_=planes[b][:, slot, :, t * CLASS_COLS:(t + 1) * CLASS_COLS].rearrange("p c (g e) -> p g c e", e=4),
+                out=rows[:].rearrange("p (g e c) -> p g c e", e=4, c=CLASSES),
+                in_=planes[q][:, :, t * CLASS_COLS:(t + 1) * CLASS_COLS].rearrange("p c (g e) -> p g c e", e=4),
             )
             r = 2 * q + t
-            nc.sync.dma_start(out=out_view[:, r * OUT_COLS:(r + 1) * OUT_COLS], in_=rows)
+            nc.sync.dma_start(out=out_view[:, r * OUT_COLS:(r + 1) * OUT_COLS], in_=rows[:])
 
         def mul(dst, left, right):
             nc.vector.tensor_tensor(out=dst, in0=left, in1=right, op=MULT)
 
+        def halved(tile_):
+            return tile_[:].rearrange("p (h n) -> p h n", h=2)
+
         def divide(b):
-            cs = cosines[b]
-            sn = sines[b]
-            half = PLANE // 2
-            quarter = PLANE // 4
-            p1 = work.tile([P, PLANE], F32, name="p1_%d" % b, tag="p1")
-            p2 = work.tile([P, half], F32, name="p2_%d" % b, tag="p2")
-            p3 = work.tile([P, quarter], F32, name="p3_%d" % b, tag="p3")
-            r3 = work.tile([P, quarter], F32, name="r3_%d" % b, tag="r3")
-            r2 = work.tile([P, half], F32, name="r2_%d" % b, tag="r2")
-            r1 = work.tile([P, PLANE], F32, name="r1_%d" % b, tag="r1")
-            num = work.tile([P, 2, PLANE], F32, name="num_%d" % b, tag="num")
-            mul(p1[:], cs[:, 0, :], cs[:, 1, :])
-            mul(num[:, 0, :], sn[:, 0, :], cs[:, 0, :])
-            mul(p2[:], p1[:, 0:half], p1[:, half:PLANE])
-            mul(num[:, 1, :], sn[:, 1, :], cs[:, 1, :])
-            mul(p3[:], p2[:, 0:quarter], p2[:, quarter:half])
-            nc.vector.reciprocal(out=r3[:], in_=p3[:])
-            mul(r2[:, 0:quarter], r3[:], p2[:, quarter:half])
-            mul(r2[:, quarter:half], r3[:], p2[:, 0:quarter])
-            mul(r1[:, 0:half], r2[:], p1[:, half:PLANE])
-            mul(r1[:, half:PLANE], r2[:], p1[:, 0:half])
-            mul(planes[b][:, :, TAN, :], num[:], r1[:].unsqueeze(1).to_broadcast([P, 2, PLANE]))
+            pairs = BATCH_PAIRS[b]
+            n = len(pairs) * PLANE
+            cs = halved(cosines[b])
+            sn = halved(sines[b])
+            p1 = work.tile([P, n // 2], F32, name="p1_%d" % b, tag="p1")
+            p2 = work.tile([P, n // 4], F32, name="p2_%d" % b, tag="p2")
+            p3 = work.tile([P, n // 8], F32, name="p3_%d" % b, tag="p3")
+            r3 = work.tile([P, n // 8], F32, name="r3_%d" % b, tag="r3")
+            r2 = work.tile([P, n // 4], F32, name="r2_%d" % b, tag="r2")
+            r1 = work.tile([P, n // 2], F32, name="r1_%d" % b, tag="r1")
+            num = work.tile([P, n], F32, name="num_%d" % b, tag="num")
+
+            def both(once):
+                return once[:].unsqueeze(1).to_broadcast([P, 2, once.shape[1]])
+
+            def finish():
+                if len(pairs) == 1:
+                    mul(halved_plane(pairs[0]), halved(num), both(r1))
+                else:
+                    for j, q in enumerate(pairs):
+                        mul(planes[q][:, TAN, :], halved(num)[:, j, :], r1[:])
+
+            return [
+                lambda: mul(p1[:], cs[:, 0, :], cs[:, 1, :]),
+                lambda: mul(halved(num)[:, 0, :], sn[:, 0, :], cs[:, 1, :]),
+                lambda: mul(p2[:], halved(p1)[:, 0, :], halved(p1)[:, 1, :]),
+                lambda: mul(p3[:], halved(p2)[:, 0, :], halved(p2)[:, 1, :]),
+                lambda: nc.vector.reciprocal(out=r3[:], in_=p3[:]),
+                lambda: mul(halved(r2), both(r3), halved(p2)[:, ::-1, :]),
+                lambda: mul(halved(num)[:, 1, :], sn[:, 1, :], cs[:, 0, :]),
+                lambda: mul(halved(r1), both(r2), halved(p1)[:, ::-1, :]),
+                finish,
+            ]
+
+        def halved_plane(q):
+            return planes[q][:, TAN, :].rearrange("p (h n) -> p h n", h=2)
+
+        GAPS_AFTER = (2, 3, 4, 5, 7)
+
+        def divide_between(b, others):
+            others = list(others)
+            for i, step in enumerate(divide(b)):
+                step()
+                if i in GAPS_AFTER and others:
+                    others.pop(0)()
+            for other in others:
+                other()
+
+        def weaves(b):
+            return [lambda q=q, t=t: weave_and_store(q, t) for q in BATCH_PAIRS[b] for t in range(2)]
 
         transpose_weight(TAN)
         transpose_x(0)
         transpose_x(1)
+        transpose_x(2)
         regroup_weight(TAN, True)
         regroup_x(0, False)
         quantise_weight(TAN)
         quantise_x(0, 1)
         multiply_tan(0)
-        transpose_x(2)
-        transpose_x(3)
-        regroup_x(1, True)
-        regroup_x(2, True)
+        regroup_x(1, False)
         quantise_x(1, 1)
         multiply_tan(1)
         transpose_weight(COS)
+        regroup_x(2, False)
+        tan_inputs(0)
+        quantise_x(2, 1)
+        multiply_tan(2)
         transpose_weight(SIN)
         transpose_weight(LINEAR)
-        tan_inputs(0)
-        regroup_x(3, True)
-        regroup_weight(COS, True)
-        quantise_x(2, 2)
-        multiply_tan(2)
-        multiply_tan(3)
-        regroup_weight(SIN, False)
-        regroup_weight(LINEAR, False)
-        quantise_weight(COS)
-        quantise_weight(SIN)
-        quantise_weight(LINEAR)
-        divide(0)
-
-        for b in range(BATCHES):
-            ahead = b + 1
-            if ahead < BATCHES:
-                tan_inputs(ahead)
-            if ahead + 1 < BATCHES:
-                transpose_x(2 * ahead + 2)
-                transpose_x(2 * ahead + 3)
-                regroup_x(2 * ahead + 2, False)
-                regroup_x(2 * ahead + 3, False)
-            multiply_rest(2 * b)
-            multiply_rest(2 * b + 1)
-            other_classes(2 * b)
-            other_classes(2 * b + 1)
-            if ahead + 1 < BATCHES:
-                quantise_x(2 * ahead + 2, 2)
-                multiply_tan(2 * ahead + 2)
-                multiply_tan(2 * ahead + 3)
-            if ahead < BATCHES:
-                divide(ahead)
-            for step in range(4):
-                weave_and_store(b, step)
+        for c in (COS, SIN, LINEAR):
+            regroup_weight(c, True)
+            quantise_weight(c)
+        transpose_x(3)
+        transpose_x(4)
+        tan_inputs(1)
+        regroup_x(3, False)
+        regroup_x(4, False)
+        multiply_rest(0)
+        divide_between(0, [lambda: quantise_x(3, 1), lambda: quantise_x(4, 1)])
+        last = len(BATCH_PAIRS) - 1
+        for b in range(last + 1):
+            if b + 2 <= last:
+                for q in BATCH_PAIRS[b + 2]:
+                    multiply_tan(q)
+            for q in BATCH_PAIRS[b]:
+                other_classes(q)
+            if b + 2 <= last:
+                tan_inputs(b + 2)
+            extra = []
+            if b + 3 <= last:
+                for q in BATCH_PAIRS[b + 3]:
+                    transpose_x(q)
+                for q in BATCH_PAIRS[b + 3]:
+                    regroup_x(q, False)
+                    extra.append(lambda q=q: quantise_x(q, 1))
+            if b < last:
+                for q in BATCH_PAIRS[b + 1]:
+                    multiply_rest(q)
+                divide_between(b + 1, weaves(b) + extra)
+            else:
+                for weave in weaves(b):
+                    weave()

@@ -20,6 +20,7 @@ ROW_WORDS = K // 2
 PACK = 4
 ROW_TILES = 16
 BATCH_PAIRS = ((0,), (1, 2), (3, 4), (5, 6), (7,))
+X_ON_VECTOR = (2, 3)
 LINEAR = 0
 COS = 1
 SIN = 2
@@ -38,7 +39,6 @@ def tile_mylayerfunc_kernel(tc, x, weight, out):
         keep = ctx.enter_context(tc.tile_pool(name="keep", bufs=1))
         work = ctx.enter_context(tc.tile_pool(name="work", bufs=2))
         psum = ctx.enter_context(tc.psum_pool(name="psum", bufs=8))
-        ctx.enter_context(tc.manual_schedule())
 
         zero = keep.tile([P, 1], F32, name="zero")
         half_pi = keep.tile([P, 1], F32, name="half_pi")
@@ -65,13 +65,15 @@ def tile_mylayerfunc_kernel(tc, x, weight, out):
             )
 
         load_weight(TAN)
-        for q in range(3):
-            load_x(2 * q, 2 * q + 2)
+        load_x(0, 2)
+        load_x(2, 4)
         load_weight(COS)
+        load_x(4, 6)
         load_weight(SIN)
         load_weight(LINEAR)
-        load_x(6, 10)
-        load_x(10, 16)
+        load_x(6, 8)
+        load_x(8, 12)
+        load_x(12, 16)
         w_words = w_raw[:].bitcast(F32)
         x_words = x_raw[:].bitcast(F32)
 
@@ -156,12 +158,16 @@ def tile_mylayerfunc_kernel(tc, x, weight, out):
         sines = {}
         planes = {}
 
+        def planes_of(q):
+            if q not in planes:
+                planes[q] = work.tile([P, CLASSES, PLANE], F32, name="res_%d" % q, tag="res", bufs=6)
+            return planes[q]
+
         def multiply_tan(q):
             y_tan[q] = multiply(q, TAN)
 
         def multiply_rest(q):
             y_rest[q] = [multiply(q, COS), multiply(q, SIN), multiply(q, LINEAR)]
-            planes[q] = work.tile([P, CLASSES, PLANE], F32, name="res_%d" % q, tag="res", bufs=6)
 
         def tan_inputs(b):
             pairs = BATCH_PAIRS[b]
@@ -175,22 +181,31 @@ def tile_mylayerfunc_kernel(tc, x, weight, out):
                 nc.scalar.activation(out=sines[b][:, cols], in_=y_tan[q][:], func=ACT.Sin)
             nc.scalar.activation(out=cosines[b][:], in_=magnitudes[:], func=ACT.Sin, scale=-1.0, bias=half_pi[:])
 
-        def other_classes(q):
+        def other_classes(q, lo=0, hi=PLANE):
             y_cos, y_sin, y_linear = y_rest[q]
-            magnitude = work.tile([P, PLANE], F32, name="abs1_%d" % q, tag="abs1")
-            nc.scalar.activation(out=magnitude[:], in_=y_cos[:], func=ACT.Abs)
-            nc.scalar.activation(out=planes[q][:, SIN, :], in_=y_sin[:], func=ACT.Sin)
-            nc.scalar.activation(out=planes[q][:, COS, :], in_=magnitude[:], func=ACT.Sin, scale=-1.0, bias=half_pi[:])
-            nc.scalar.copy(out=planes[q][:, LINEAR, :], in_=y_linear[:])
-
-        def weave_and_store(q, t):
-            rows = work.tile([P, OUT_COLS], F32, name="o_%d_%d" % (q, t), tag="o", bufs=6)
-            nc.vector.tensor_copy(
-                out=rows[:].rearrange("p (g e c) -> p g c e", e=4, c=CLASSES),
-                in_=planes[q][:, :, t * CLASS_COLS:(t + 1) * CLASS_COLS].rearrange("p c (g e) -> p g c e", e=4),
+            cols = slice(lo, hi)
+            magnitude = work.tile([P, PLANE], F32, name="abs1_%d_%d" % (q, lo), tag="abs1")
+            nc.scalar.activation(out=magnitude[:, cols], in_=y_cos[:, cols], func=ACT.Abs)
+            nc.scalar.activation(out=planes_of(q)[:, SIN, cols], in_=y_sin[:, cols], func=ACT.Sin)
+            nc.scalar.activation(
+                out=planes_of(q)[:, COS, cols], in_=magnitude[:, cols], func=ACT.Sin, scale=-1.0, bias=half_pi[:]
             )
-            r = 2 * q + t
-            nc.sync.dma_start(out=out_view[:, r * OUT_COLS:(r + 1) * OUT_COLS], in_=rows[:])
+            nc.scalar.copy(out=planes_of(q)[:, LINEAR, cols], in_=y_linear[:, cols])
+
+        def weave_and_store(q, t, pieces=1):
+            rows = work.tile([P, OUT_COLS], F32, name="o_%d_%d" % (q, t), tag="o", bufs=6)
+            first = (2 * q + t) * OUT_COLS
+            n = CLASS_COLS // pieces
+            for i in range(pieces):
+                lo = t * CLASS_COLS + i * n
+                part = rows[:, i * CLASSES * n:(i + 1) * CLASSES * n]
+                nc.vector.tensor_copy(
+                    out=part.rearrange("p (g e c) -> p g c e", e=4, c=CLASSES),
+                    in_=planes[q][:, :, lo:lo + n].rearrange("p c (g e) -> p g c e", e=4),
+                )
+                nc.sync.dma_start(
+                    out=out_view[:, first + i * CLASSES * n:first + (i + 1) * CLASSES * n], in_=part
+                )
 
         def mul(dst, left, right):
             nc.vector.tensor_tensor(out=dst, in0=left, in1=right, op=MULT)
@@ -219,86 +234,102 @@ def tile_mylayerfunc_kernel(tc, x, weight, out):
                     mul(halved_plane(pairs[0]), halved(num), both(r1))
                 else:
                     for j, q in enumerate(pairs):
-                        mul(planes[q][:, TAN, :], halved(num)[:, j, :], r1[:])
+                        mul(planes_of(q)[:, TAN, :], halved(num)[:, j, :], r1[:])
 
-            return [
-                lambda: mul(p1[:], cs[:, 0, :], cs[:, 1, :]),
+            numerators = [
                 lambda: mul(halved(num)[:, 0, :], sn[:, 0, :], cs[:, 1, :]),
+                lambda: mul(halved(num)[:, 1, :], sn[:, 1, :], cs[:, 0, :]),
+            ]
+            steps = [
+                lambda: mul(p1[:], cs[:, 0, :], cs[:, 1, :]),
                 lambda: mul(p2[:], halved(p1)[:, 0, :], halved(p1)[:, 1, :]),
                 lambda: mul(p3[:], halved(p2)[:, 0, :], halved(p2)[:, 1, :]),
                 lambda: nc.vector.reciprocal(out=r3[:], in_=p3[:]),
                 lambda: mul(halved(r2), both(r3), halved(p2)[:, ::-1, :]),
-                lambda: mul(halved(num)[:, 1, :], sn[:, 1, :], cs[:, 0, :]),
                 lambda: mul(halved(r1), both(r2), halved(p1)[:, ::-1, :]),
                 finish,
             ]
+            return numerators, steps
 
         def halved_plane(q):
-            return planes[q][:, TAN, :].rearrange("p (h n) -> p h n", h=2)
-
-        GAPS_AFTER = (2, 3, 4, 5, 7)
+            return planes_of(q)[:, TAN, :].rearrange("p (h n) -> p h n", h=2)
 
         def divide_between(b, others):
-            others = list(others)
-            for i, step in enumerate(divide(b)):
+            numerators, steps = divide(b)
+            others = numerators + list(others)
+            for i, step in enumerate(steps):
                 step()
-                if i in GAPS_AFTER and others:
+                if i + 1 < len(steps) and others:
                     others.pop(0)()
-            for other in others:
-                other()
+            return others
 
         def weaves(b):
             return [lambda q=q, t=t: weave_and_store(q, t) for q in BATCH_PAIRS[b] for t in range(2)]
 
+        ctx.enter_context(tc.manual_schedule())
         transpose_weight(TAN)
         transpose_x(0)
         transpose_x(1)
-        transpose_x(2)
+        transpose_weight(COS)
         regroup_weight(TAN, True)
         regroup_x(0, False)
         quantise_weight(TAN)
         quantise_x(0, 1)
         multiply_tan(0)
+        transpose_x(2)
         regroup_x(1, False)
+        regroup_weight(COS, True)
         quantise_x(1, 1)
         multiply_tan(1)
-        transpose_weight(COS)
-        regroup_x(2, False)
+        transpose_weight(SIN)
+        regroup_x(2, True)
         tan_inputs(0)
+        transpose_weight(LINEAR)
+        quantise_weight(COS)
         quantise_x(2, 1)
         multiply_tan(2)
-        transpose_weight(SIN)
-        transpose_weight(LINEAR)
-        for c in (COS, SIN, LINEAR):
-            regroup_weight(c, True)
-            quantise_weight(c)
-        transpose_x(3)
-        transpose_x(4)
+        regroup_weight(SIN, True)
+        for q in BATCH_PAIRS[2]:
+            transpose_x(q)
+        regroup_weight(LINEAR, True)
+        quantise_weight(SIN)
+        fillers = [lambda: quantise_weight(LINEAR)]
         tan_inputs(1)
-        regroup_x(3, False)
-        regroup_x(4, False)
+        for q in BATCH_PAIRS[2]:
+            regroup_x(q, q in X_ON_VECTOR)
+            fillers.append(lambda q=q: quantise_x(q, 1))
+        rest = divide_between(0, fillers)
         multiply_rest(0)
-        divide_between(0, [lambda: quantise_x(3, 1), lambda: quantise_x(4, 1)])
+        for other in rest:
+            other()
         last = len(BATCH_PAIRS) - 1
         for b in range(last + 1):
             if b + 2 <= last:
                 for q in BATCH_PAIRS[b + 2]:
                     multiply_tan(q)
             for q in BATCH_PAIRS[b]:
-                other_classes(q)
-            if b + 2 <= last:
-                tan_inputs(b + 2)
-            extra = []
+                if b < last:
+                    other_classes(q)
+                else:
+                    other_classes(q, 0, CLASS_COLS)
+                    other_classes(q, CLASS_COLS, PLANE)
             if b + 3 <= last:
                 for q in BATCH_PAIRS[b + 3]:
                     transpose_x(q)
+            if b + 2 <= last:
+                tan_inputs(b + 2)
+            fillers = []
+            if b < last:
+                fillers.extend(weaves(b))
+            if b + 3 <= last:
                 for q in BATCH_PAIRS[b + 3]:
                     regroup_x(q, False)
-                    extra.append(lambda q=q: quantise_x(q, 1))
+                    fillers.append(lambda q=q: quantise_x(q, 1))
             if b < last:
                 for q in BATCH_PAIRS[b + 1]:
                     multiply_rest(q)
-                divide_between(b + 1, weaves(b) + extra)
+                for other in divide_between(b + 1, fillers):
+                    other()
             else:
-                for weave in weaves(b):
-                    weave()
+                weave_and_store(BATCH_PAIRS[b][-1], 0)
+                weave_and_store(BATCH_PAIRS[b][-1], 1, pieces=2)

@@ -59,13 +59,18 @@ def tile_mylayerfunc_kernel(tc, x, weight, out):
                 out=w_raw[:, c * 2 * K:(c + 1) * 2 * K].rearrange("p (h k) -> p h k", h=2), in_=w_view[c]
             )
 
+        def load_weight_half(c, h):
+            nc.sync.dma_start(out=w_raw[:, (2 * c + h) * K:(2 * c + h + 1) * K], in_=w_view[c][:, h, :])
+
         def load_x(first_tile, end_tile):
             nc.sync.dma_start(
                 out=x_raw[:, first_tile * K:end_tile * K], in_=x_view[:, first_tile * K:end_tile * K]
             )
 
-        load_weight(TAN)
-        load_x(0, 2)
+        for h in range(2):
+            load_weight_half(TAN, h)
+        for t in range(2):
+            load_x(t, t + 1)
         load_x(2, 4)
         load_weight(COS)
         load_x(4, 6)
@@ -99,11 +104,19 @@ def tile_mylayerfunc_kernel(tc, x, weight, out):
 
         def regroup(on_vector, bank, dst_words):
             dst = dst_words.rearrange("p (n u) -> p n u", u=2)
-            src = bank[:].rearrange("p (u n) -> p n u", u=2)
+            src = bank.rearrange("p (u n) -> p n u", u=2)
             if on_vector:
                 nc.vector.tensor_copy(out=dst, in_=src)
             else:
                 nc.scalar.copy(out=dst, in_=src)
+
+        def transpose_block(words, first_word, label):
+            bank = psum.tile([P, BANK], F32, name=label, tag="bank")
+            for u in range(2):
+                nc.tensor.transpose(
+                    bank[:, u * P:(u + 1) * P], words[:, first_word + u:first_word + ROW_WORDS:2], ident[:]
+                )
+            return bank[:, 0:2 * P]
 
         w_banks = {}
         x_banks = {}
@@ -115,10 +128,10 @@ def tile_mylayerfunc_kernel(tc, x, weight, out):
             x_banks[q] = transpose_to_bank(x_words, q * 2 * ROW_WORDS, "xt%d" % q)
 
         def regroup_weight(c, on_vector):
-            regroup(on_vector, w_banks[c], w_grp_words[:, c * BANK:(c + 1) * BANK])
+            regroup(on_vector, w_banks[c][:], w_grp_words[:, c * BANK:(c + 1) * BANK])
 
         def regroup_x(q, on_vector):
-            regroup(on_vector, x_banks[q], x_grp_words[:, q * BANK:(q + 1) * BANK])
+            regroup(on_vector, x_banks[q][:], x_grp_words[:, q * BANK:(q + 1) * BANK])
 
         def quantise_weight(c):
             nc.vector.quantize_mx(
@@ -266,13 +279,17 @@ def tile_mylayerfunc_kernel(tc, x, weight, out):
         def weaves(b):
             return [lambda q=q, t=t: weave_and_store(q, t) for q in BATCH_PAIRS[b] for t in range(2)]
 
-        ctx.enter_context(tc.manual_schedule())
-        transpose_weight(TAN)
-        transpose_x(0)
+        w_blocks = [
+            transpose_block(w_words, (2 * TAN + h) * ROW_WORDS, "wt%d_%d" % (TAN, h)) for h in range(2)
+        ]
+        x_blocks = [transpose_block(x_words, t * ROW_WORDS, "xt0_%d" % t) for t in range(2)]
         transpose_x(1)
         transpose_weight(COS)
-        regroup_weight(TAN, True)
-        regroup_x(0, False)
+        for h in range(2):
+            first = (2 * TAN + h) * ROW_WORDS
+            regroup(h == 0, w_blocks[h], w_grp_words[:, first:first + ROW_WORDS])
+        for t in range(2):
+            regroup(t == 0, x_blocks[t], x_grp_words[:, t * ROW_WORDS:(t + 1) * ROW_WORDS])
         quantise_weight(TAN)
         quantise_x(0, 1)
         multiply_tan(0)

@@ -21,6 +21,7 @@ PACK = 4
 ROW_TILES = 16
 BATCH_PAIRS = ((0,), (1, 2), (3, 4), (5, 6), (7,))
 X_ON_VECTOR = (2, 3)
+LEVELS = {1: 3, 2: 4}
 LINEAR = 0
 COS = 1
 SIN = 2
@@ -205,20 +206,23 @@ def tile_mylayerfunc_kernel(tc, x, weight, out):
             )
             nc.scalar.copy(out=planes_of(q)[:, LINEAR, cols], in_=y_linear[:, cols])
 
-        def weave_and_store(q, t, pieces=1):
+        def weave_and_store(q, t, stores):
             rows = work.tile([P, OUT_COLS], F32, name="o_%d_%d" % (q, t), tag="o", bufs=6)
+            n = CLASS_COLS // 2
             first = (2 * q + t) * OUT_COLS
-            n = CLASS_COLS // pieces
-            for i in range(pieces):
-                lo = t * CLASS_COLS + i * n
-                part = rows[:, i * CLASSES * n:(i + 1) * CLASSES * n]
+
+            def weave(h):
+                lo = t * CLASS_COLS + h * n
                 nc.vector.tensor_copy(
-                    out=part.rearrange("p (g e c) -> p g c e", e=4, c=CLASSES),
-                    in_=planes[q][:, :, lo:lo + n].rearrange("p c (g e) -> p g c e", e=4),
+                    out=rows[:, h * CLASSES * n:(h + 1) * CLASSES * n].rearrange("p (g e c) -> p g c e", e=4, c=CLASSES),
+                    in_=planes_of(q)[:, :, lo:lo + n].rearrange("p c (g e) -> p g c e", e=4),
                 )
-                nc.sync.dma_start(
-                    out=out_view[:, first + i * CLASSES * n:first + (i + 1) * CLASSES * n], in_=part
-                )
+                if stores == 2 or h == 1:
+                    start = h * CLASSES * n if stores == 2 else 0
+                    end = (h + 1) * CLASSES * n
+                    nc.sync.dma_start(out=out_view[:, first + start:first + end], in_=rows[:, start:end])
+
+            return [lambda: weave(0), lambda: weave(1)]
 
         def mul(dst, left, right):
             nc.vector.tensor_tensor(out=dst, in0=left, in1=right, op=MULT)
@@ -231,37 +235,39 @@ def tile_mylayerfunc_kernel(tc, x, weight, out):
             n = len(pairs) * PLANE
             cs = halved(cosines[b])
             sn = halved(sines[b])
-            p1 = work.tile([P, n // 2], F32, name="p1_%d" % b, tag="p1")
-            p2 = work.tile([P, n // 4], F32, name="p2_%d" % b, tag="p2")
-            p3 = work.tile([P, n // 8], F32, name="p3_%d" % b, tag="p3")
-            r3 = work.tile([P, n // 8], F32, name="r3_%d" % b, tag="r3")
-            r2 = work.tile([P, n // 4], F32, name="r2_%d" % b, tag="r2")
-            r1 = work.tile([P, n // 2], F32, name="r1_%d" % b, tag="r1")
+            levels = LEVELS[len(pairs)]
             num = work.tile([P, n], F32, name="num_%d" % b, tag="num")
+            products = [cosines[b]]
+            for v in range(1, levels + 1):
+                products.append(work.tile([P, n >> v], F32, name="p%d_%d" % (v, b), tag="p%d" % v))
+            inverses = {}
+            for v in range(1, levels + 1):
+                inverses[v] = work.tile([P, n >> v], F32, name="r%d_%d" % (v, b), tag="r%d" % v)
 
             def both(once):
                 return once[:].unsqueeze(1).to_broadcast([P, 2, once.shape[1]])
 
+            def up(v):
+                mul(products[v][:], halved(products[v - 1])[:, 0, :], halved(products[v - 1])[:, 1, :])
+
+            def down(v):
+                mul(halved(inverses[v]), both(inverses[v + 1]), halved(products[v])[:, ::-1, :])
+
             def finish():
                 if len(pairs) == 1:
-                    mul(halved_plane(pairs[0]), halved(num), both(r1))
+                    mul(halved_plane(pairs[0]), halved(num), both(inverses[1]))
                 else:
                     for j, q in enumerate(pairs):
-                        mul(planes_of(q)[:, TAN, :], halved(num)[:, j, :], r1[:])
+                        mul(planes_of(q)[:, TAN, :], halved(num)[:, j, :], inverses[1][:])
 
             numerators = [
                 lambda: mul(halved(num)[:, 0, :], sn[:, 0, :], cs[:, 1, :]),
                 lambda: mul(halved(num)[:, 1, :], sn[:, 1, :], cs[:, 0, :]),
             ]
-            steps = [
-                lambda: mul(p1[:], cs[:, 0, :], cs[:, 1, :]),
-                lambda: mul(p2[:], halved(p1)[:, 0, :], halved(p1)[:, 1, :]),
-                lambda: mul(p3[:], halved(p2)[:, 0, :], halved(p2)[:, 1, :]),
-                lambda: nc.vector.reciprocal(out=r3[:], in_=p3[:]),
-                lambda: mul(halved(r2), both(r3), halved(p2)[:, ::-1, :]),
-                lambda: mul(halved(r1), both(r2), halved(p1)[:, ::-1, :]),
-                finish,
-            ]
+            steps = [lambda v=v: up(v) for v in range(1, levels + 1)]
+            steps.append(lambda: nc.vector.reciprocal(out=inverses[levels][:], in_=products[levels][:]))
+            steps.extend([lambda v=v: down(v) for v in range(levels - 1, 0, -1)])
+            steps.append(finish)
             return numerators, steps
 
         def halved_plane(q):
@@ -277,7 +283,11 @@ def tile_mylayerfunc_kernel(tc, x, weight, out):
             return others
 
         def weaves(b):
-            return [lambda q=q, t=t: weave_and_store(q, t) for q in BATCH_PAIRS[b] for t in range(2)]
+            pieces = []
+            for q in BATCH_PAIRS[b]:
+                for t in range(2):
+                    pieces.extend(weave_and_store(q, t, 2 if 2 * q + t == ROW_TILES - 1 else 1))
+            return pieces
 
         w_blocks = [
             transpose_block(w_words, (2 * TAN + h) * ROW_WORDS, "wt%d_%d" % (TAN, h)) for h in range(2)
@@ -348,5 +358,5 @@ def tile_mylayerfunc_kernel(tc, x, weight, out):
                 for other in divide_between(b + 1, fillers):
                     other()
             else:
-                weave_and_store(BATCH_PAIRS[b][-1], 0)
-                weave_and_store(BATCH_PAIRS[b][-1], 1, pieces=2)
+                for piece in weaves(b):
+                    piece()

@@ -207,7 +207,7 @@ def tile_mylayerfunc_kernel(tc, x, weight, out):
             nc.scalar.copy(out=planes_of(q)[:, LINEAR, cols], in_=y_linear[:, cols])
 
         def weave_and_store(q, t, stores):
-            rows = work.tile([P, OUT_COLS], F32, name="o_%d_%d" % (q, t), tag="o", bufs=6)
+            rows = work.tile([P, OUT_COLS], F32, name="o_%d_%d" % (q, t), tag="o", bufs=12)
             n = CLASS_COLS // 2
             first = (2 * q + t) * OUT_COLS
 
@@ -335,6 +335,8 @@ def tile_mylayerfunc_kernel(tc, x, weight, out):
                 for q in BATCH_PAIRS[b + 2]:
                     multiply_tan(q)
             for q in BATCH_PAIRS[b]:
+                if b == last - 1 and q == BATCH_PAIRS[b][-1]:
+                    tan_inputs(last)
                 if b < last:
                     other_classes(q)
                 else:
@@ -343,7 +345,7 @@ def tile_mylayerfunc_kernel(tc, x, weight, out):
             if b + 3 <= last:
                 for q in BATCH_PAIRS[b + 3]:
                     transpose_x(q)
-            if b + 2 <= last:
+            if b + 2 < last:
                 tan_inputs(b + 2)
             fillers = []
             if b < last:

@@ -214,8 +214,8 @@ def tile_mylayerfunc_kernel(tc, x, weight, out):
             def weave(h):
                 lo = t * CLASS_COLS + h * n
                 nc.vector.tensor_copy(
-                    out=rows[:, h * CLASSES * n:(h + 1) * CLASSES * n].rearrange("p (g e c) -> p g c e", e=4, c=CLASSES),
-                    in_=planes_of(q)[:, :, lo:lo + n].rearrange("p c (g e) -> p g c e", e=4),
+                    out=rows[:, h * CLASSES * n:(h + 1) * CLASSES * n].rearrange("p (g e c) -> p g c e", e=2, c=CLASSES),
+                    in_=planes_of(q)[:, :, lo:lo + n].rearrange("p c (g e) -> p g c e", e=2),
                 )
                 if stores == 2 or h == 1:
                     start = h * CLASSES * n if stores == 2 else 0

import math
from contextlib import ExitStack

import concourse.mybir as mybir
from concourse.masks import make_identity

FLOPS = 2 * 2048 * 512 * 1024

F32 = mybir.dt.float32
BF16 = mybir.dt.bfloat16
U32 = mybir.dt.uint32
U8 = mybir.dt.uint8
FP8X4 = mybir.dt.float8_e4m3fn_x4
ACT = mybir.ActivationFunctionType
MULT = mybir.AluOpType.mult

P = 128
K = 512
ROW_WORDS = K // 2
PACK = 4
ROW_TILES = 16
BATCH_PAIRS = ((0,), (1, 2), (3, 4), (5, 6), (7,))
X_ON_VECTOR = (2, 3)
LEVELS = {1: 3, 2: 4}
LINEAR = 0
COS = 1
SIN = 2
TAN = 3
CLASSES = 4
CLASS_COLS = 256
OUT_COLS = CLASSES * CLASS_COLS
PLANE = 2 * CLASS_COLS
BANK = 512
assert PLANE == BANK


def tile_mylayerfunc_kernel(tc, x, weight, out):
    nc = tc.nc
    with ExitStack() as ctx:
        keep = ctx.enter_context(tc.tile_pool(name="keep", bufs=1))
        work = ctx.enter_context(tc.tile_pool(name="work", bufs=2))
        psum = ctx.enter_context(tc.psum_pool(name="psum", bufs=8))

        zero = keep.tile([P, 1], F32, name="zero")
        half_pi = keep.tile([P, 1], F32, name="half_pi")
        warm = keep.tile([P, 1], F32, name="warm")
        ident = keep.tile([P, P], F32, name="ident")
        nc.vector.memset(zero[:], 0.0)
        nc.vector.tensor_scalar_add(out=half_pi[:], in0=zero[:], scalar1=math.pi / 2)
        nc.scalar.activation(out=warm[:], in_=half_pi[:], func=ACT.Sin)
        make_identity(nc, ident[:])

        w_raw = keep.tile([P, CLASSES * 2 * K], BF16, name="w_raw")
        x_raw = keep.tile([P, ROW_TILES * K], BF16, name="x_raw")
        w_view = weight.rearrange("(h p c) k -> c p h k", h=2, p=P, c=CLASSES)
        x_view = x.rearrange("(p r) k -> p (r k)", r=ROW_TILES)

        def load_weight(c):
            nc.sync.dma_start(
                out=w_raw[:, c * 2 * K:(c + 1) * 2 * K].rearrange("p (h k) -> p h k", h=2), in_=w_view[c]
            )

        def load_weight_half(c, h):
            nc.sync.dma_start(out=w_raw[:, (2 * c + h) * K:(2 * c + h + 1) * K], in_=w_view[c][:, h, :])

        def load_x(first_tile, end_tile):
            nc.sync.dma_start(
                out=x_raw[:, first_tile * K:end_tile * K], in_=x_view[:, first_tile * K:end_tile * K]
            )

        for h in range(2):
            load_weight_half(TAN, h)
        for t in range(2):
            load_x(t, t + 1)
        load_x(2, 4)
        load_weight(COS)
        load_x(4, 6)
        load_weight(SIN)
        load_weight(LINEAR)
        load_x(6, 8)
        load_x(8, 12)
        load_x(12, 16)
        w_words = w_raw[:].bitcast(F32)
        x_words = x_raw[:].bitcast(F32)

        w_grp = keep.tile([P, OUT_COLS * PACK], BF16, name="w_grp", align_bytes=64)
        x_grp = keep.tile([P, ROW_TILES * P * PACK], BF16, name="x_grp", align_bytes=64)
        w_grp_words = w_grp[:].bitcast(F32)
        x_grp_words = x_grp[:].bitcast(F32)
        w_codes = keep.tile([P, OUT_COLS], U32, name="w_codes", align_bytes=64)
        w_scales = keep.tile([P, OUT_COLS], U8, name="w_scales", align_bytes=64)
        x_codes = keep.tile([P, ROW_TILES * P], U32, name="x_codes", align_bytes=64)
        x_scales = keep.tile([P, ROW_TILES * P], U8, name="x_scales", align_bytes=64)

        def transpose_to_bank(words, first_word, label):
            bank = psum.tile([P, BANK], F32, name=label, tag="bank")
            halves = bank[:].rearrange("p (u n) -> p u n", u=2)
            for blk in range(2):
                for u in range(2):
                    lo = first_word + blk * ROW_WORDS
                    nc.tensor.transpose(
                        halves[:, u, blk * P:(blk + 1) * P], words[:, lo + u:lo + ROW_WORDS:2], ident[:]
                    )
            return bank

        def regroup(on_vector, bank, dst_words):
            dst = dst_words.rearrange("p (n u) -> p n u", u=2)
            src = bank.rearrange("p (u n) -> p n u", u=2)
            if on_vector:
                nc.vector.tensor_copy(out=dst, in_=src)
            else:
                nc.scalar.copy(out=dst, in_=src)

        def transpose_block(words, first_word, label):
            bank = psum.tile([P, BANK], F32, name=label, tag="bank")
            for u in range(2):
                nc.tensor.transpose(
                    bank[:, u * P:(u + 1) * P], words[:, first_word + u:first_word + ROW_WORDS:2], ident[:]
                )
            return bank[:, 0:2 * P]

        w_banks = {}
        x_banks = {}

        def transpose_weight(c):
            w_banks[c] = transpose_to_bank(w_words, c * 2 * ROW_WORDS, "wt%d" % c)

        def transpose_x(q):
            x_banks[q] = transpose_to_bank(x_words, q * 2 * ROW_WORDS, "xt%d" % q)

        def regroup_weight(c, on_vector):
            regroup(on_vector, w_banks[c][:], w_grp_words[:, c * BANK:(c + 1) * BANK])

        def regroup_x(q, on_vector):
            regroup(on_vector, x_banks[q][:], x_grp_words[:, q * BANK:(q + 1) * BANK])

        def quantise_weight(c):
            nc.vector.quantize_mx(
                out=w_codes[:, c * CLASS_COLS:(c + 1) * CLASS_COLS].bitcast(FP8X4),
                scales=w_scales[:, c * CLASS_COLS:(c + 1) * CLASS_COLS],
                in_=w_grp[:, c * CLASS_COLS * PACK:(c + 1) * CLASS_COLS * PACK],
            )

        def quantise_x(first_pair, pairs):
            lo = first_pair * 2 * P
            hi = (first_pair + pairs) * 2 * P
            nc.vector.quantize_mx(
                out=x_codes[:, lo:hi].bitcast(FP8X4),
                scales=x_scales[:, lo:hi],
                in_=x_grp[:, PACK * lo:PACK * hi],
            )

        def multiply(q, c):
            bank = psum.tile([P, BANK], F32, name="y%d_%d" % (c, q), tag="bank")
            for t in range(2):
                r = 2 * q + t
                nc.tensor.matmul_mx(
                    out=bank[:, t * CLASS_COLS:(t + 1) * CLASS_COLS],
                    lhsT=x_codes[:, r * P:(r + 1) * P].bitcast(FP8X4),
                    lhsT_scale=x_scales[:, r * P:(r + 1) * P],
                    rhs=w_codes[:, c * CLASS_COLS:(c + 1) * CLASS_COLS].bitcast(FP8X4),
                    rhs_scale=w_scales[:, c * CLASS_COLS:(c + 1) * CLASS_COLS],
                    start=True,
                    stop=True,
                )
            return bank

        out_view = out.rearrange("(p r) j -> p (r j)", r=ROW_TILES)
        y_tan = {}
        y_rest = {}
        cosines = {}
        sines = {}
        planes = {}

        def planes_of(q):
            if q not in planes:
                planes[q] = work.tile([P, CLASSES, PLANE], F32, name="res_%d" % q, tag="res", bufs=6)
            return planes[q]

        def multiply_tan(q):
            y_tan[q] = multiply(q, TAN)

        def multiply_rest(q):
            y_rest[q] = [multiply(q, COS), multiply(q, SIN), multiply(q, LINEAR)]

        def tan_inputs(b):
            pairs = BATCH_PAIRS[b]
            n = len(pairs) * PLANE
            cosines[b] = work.tile([P, n], F32, name="cos3_%d" % b, tag="cos3")
            sines[b] = work.tile([P, n], F32, name="sin3_%d" % b, tag="sin3")
            magnitudes = work.tile([P, n], F32, name="abs3_%d" % b, tag="abs3")
            for j, q in enumerate(pairs):
                cols = slice(j * PLANE, (j + 1) * PLANE)
                nc.scalar.activation(out=magnitudes[:, cols], in_=y_tan[q][:], func=ACT.Abs)
                nc.scalar.activation(out=sines[b][:, cols], in_=y_tan[q][:], func=ACT.Sin)
            nc.scalar.activation(out=cosines[b][:], in_=magnitudes[:], func=ACT.Sin, scale=-1.0, bias=half_pi[:])

        def other_classes(q, lo=0, hi=PLANE):
            y_cos, y_sin, y_linear = y_rest[q]
            cols = slice(lo, hi)
            magnitude = work.tile([P, PLANE], F32, name="abs1_%d_%d" % (q, lo), tag="abs1")
            nc.scalar.activation(out=magnitude[:, cols], in_=y_cos[:, cols], func=ACT.Abs)
            nc.scalar.activation(out=planes_of(q)[:, SIN, cols], in_=y_sin[:, cols], func=ACT.Sin)
            nc.scalar.activation(
                out=planes_of(q)[:, COS, cols], in_=magnitude[:, cols], func=ACT.Sin, scale=-1.0, bias=half_pi[:]
            )
            nc.scalar.copy(out=planes_of(q)[:, LINEAR, cols], in_=y_linear[:, cols])

        def weave_and_store(q, t, stores):
            rows = work.tile([P, OUT_COLS], F32, name="o_%d_%d" % (q, t), tag="o", bufs=12)
            n = CLASS_COLS // 2
            first = (2 * q + t) * OUT_COLS

            def weave(h):
                lo = t * CLASS_COLS + h * n
                nc.vector.tensor_copy(
                    out=rows[:, h * CLASSES * n:(h + 1) * CLASSES * n].rearrange("p (g e c) -> p g c e", e=2, c=CLASSES),
                    in_=planes_of(q)[:, :, lo:lo + n].rearrange("p c (g e) -> p g c e", e=2),
                )
                if stores == 2 or h == 1:
                    start = h * CLASSES * n if stores == 2 else 0
                    end = (h + 1) * CLASSES * n
                    nc.sync.dma_start(out=out_view[:, first + start:first + end], in_=rows[:, start:end])

            return [lambda: weave(0), lambda: weave(1)]

        def mul(dst, left, right):
            nc.vector.tensor_tensor(out=dst, in0=left, in1=right, op=MULT)

        def halved(tile_):
            return tile_[:].rearrange("p (h n) -> p h n", h=2)

        def divide(b):
            pairs = BATCH_PAIRS[b]
            n = len(pairs) * PLANE
            cs = halved(cosines[b])
            sn = halved(sines[b])
            levels = LEVELS[len(pairs)]
            num = work.tile([P, n], F32, name="num_%d" % b, tag="num")
            products = [cosines[b]]
            for v in range(1, levels + 1):
                products.append(work.tile([P, n >> v], F32, name="p%d_%d" % (v, b), tag="p%d" % v))
            inverses = {}
            for v in range(1, levels + 1):
                inverses[v] = work.tile([P, n >> v], F32, name="r%d_%d" % (v, b), tag="r%d" % v)

            def both(once):
                return once[:].unsqueeze(1).to_broadcast([P, 2, once.shape[1]])

            def up(v):
                mul(products[v][:], halved(products[v - 1])[:, 0, :], halved(products[v - 1])[:, 1, :])

            def down(v):
                mul(halved(inverses[v]), both(inverses[v + 1]), halved(products[v])[:, ::-1, :])

            def finish():
                if len(pairs) == 1:
                    mul(halved_plane(pairs[0]), halved(num), both(inverses[1]))
                else:
                    for j, q in enumerate(pairs):
                        mul(planes_of(q)[:, TAN, :], halved(num)[:, j, :], inverses[1][:])

            numerators = [
                lambda: mul(halved(num)[:, 0, :], sn[:, 0, :], cs[:, 1, :]),
                lambda: mul(halved(num)[:, 1, :], sn[:, 1, :], cs[:, 0, :]),
            ]
            steps = [lambda v=v: up(v) for v in range(1, levels + 1)]
            steps.append(lambda: nc.vector.reciprocal(out=inverses[levels][:], in_=products[levels][:]))
            steps.extend([lambda v=v: down(v) for v in range(levels - 1, 0, -1)])
            steps.append(finish)
            return numerators, steps

        def halved_plane(q):
            return planes_of(q)[:, TAN, :].rearrange("p (h n) -> p h n", h=2)

        def divide_between(b, others):
            numerators, steps = divide(b)
            others = numerators + list(others)
            for i, step in enumerate(steps):
                step()
                if i + 1 < len(steps) and others:
                    others.pop(0)()
            return others

        def weaves(b):
            pieces = []
            for q in BATCH_PAIRS[b]:
                for t in range(2):
                    pieces.extend(weave_and_store(q, t, 2 if 2 * q + t == ROW_TILES - 1 else 1))
            return pieces

        w_blocks = [
            transpose_block(w_words, (2 * TAN + h) * ROW_WORDS, "wt%d_%d" % (TAN, h)) for h in range(2)
        ]
        x_blocks = [transpose_block(x_words, t * ROW_WORDS, "xt0_%d" % t) for t in range(2)]
        transpose_x(1)
        transpose_weight(COS)
        for h in range(2):
            first = (2 * TAN + h) * ROW_WORDS
            regroup(h == 0, w_blocks[h], w_grp_words[:, first:first + ROW_WORDS])
        for t in range(2):
            regroup(t == 0, x_blocks[t], x_grp_words[:, t * ROW_WORDS:(t + 1) * ROW_WORDS])
        quantise_weight(TAN)
        quantise_x(0, 1)
        multiply_tan(0)
        transpose_x(2)
        regroup_x(1, False)
        regroup_weight(COS, True)
        quantise_x(1, 1)
        multiply_tan(1)
        transpose_weight(SIN)
        regroup_x(2, True)
        tan_inputs(0)
        transpose_weight(LINEAR)
        quantise_weight(COS)
        quantise_x(2, 1)
        multiply_tan(2)
        regroup_weight(SIN, True)
        for q in BATCH_PAIRS[2]:
            transpose_x(q)
        regroup_weight(LINEAR, True)
        quantise_weight(SIN)
        fillers = [lambda: quantise_weight(LINEAR)]
        tan_inputs(1)
        for q in BATCH_PAIRS[2]:
            regroup_x(q, q in X_ON_VECTOR)
            fillers.append(lambda q=q: quantise_x(q, 1))
        rest = divide_between(0, fillers)
        multiply_rest(0)
        for other in rest:
            other()
        last = len(BATCH_PAIRS) - 1
        for b in range(last + 1):
            if b + 2 <= last:
                for q in BATCH_PAIRS[b + 2]:
                    multiply_tan(q)
            for q in BATCH_PAIRS[b]:
                if b == last - 1 and q == BATCH_PAIRS[b][-1]:
                    tan_inputs(last)
                if b < last:
                    other_classes(q)
                else:
                    other_classes(q, 0, CLASS_COLS)
                    other_classes(q, CLASS_COLS, PLANE)
            if b + 3 <= last:
                for q in BATCH_PAIRS[b + 3]:
                    transpose_x(q)
            if b + 2 < last:
                tan_inputs(b + 2)
            fillers = []
            if b < last:
                fillers.extend(weaves(b))
            if b + 3 <= last:
                for q in BATCH_PAIRS[b + 3]:
                    regroup_x(q, False)
                    fillers.append(lambda q=q: quantise_x(q, 1))
            if b < last:
                for q in BATCH_PAIRS[b + 1]:
                    multiply_rest(q)
                for other in divide_between(b + 1, fillers):
                    other()
            else:
                for piece in weaves(b):
                    piece()
